import numpy as np
import ml_dtypes


def mxq(x, axis, fmt="e4m3"):
    dtype, down = {"e4m3": (ml_dtypes.float8_e4m3fn, 7), "e5m2": (ml_dtypes.float8_e5m2, 14)}[fmt]
    v = np.moveaxis(np.asarray(x, np.float32).astype(ml_dtypes.bfloat16).astype(np.float64), axis, -1)
    blocks = v.reshape(v.shape[:-1] + (-1, 32))
    amax = np.abs(blocks).max(-1, keepdims=True)
    byte = np.maximum(np.where(amax > 0, np.frexp(amax)[1] - 1 + 127, 0) - down, 1)
    scale = np.exp2(byte - 127.0)
    codes = (blocks / scale).astype(np.float32).astype(dtype).astype(np.float64)
    return np.moveaxis((codes * scale).reshape(v.shape), -1, axis)


WIDE = False


def mx_kscale(k):
    if not WIDE:
        return np.ones(k)
    levels = np.array([10, -10, 5, -5, 0])
    if k % 512:
        return np.exp2(np.random.permutation(np.resize(levels, k // 32))).repeat(32)
    a = np.empty((k // 512, 16))
    for p in range(k // 512):
        a[p, :8] = np.random.permutation(np.resize(levels, 8))
        for g in range(8):
            far = levels[np.abs(levels - a[p, g]) >= 10]
            a[p, g + 8] = far[np.random.randint(len(far))]
    return np.exp2(a.ravel()).repeat(32)


BF16 = ml_dtypes.bfloat16


def bf(x):
    return np.asarray(x, np.float32).astype(BF16)


def f64(x):
    return np.asarray(x).astype(np.float64)


B, T, E, H, FF = 4, 1024, 1024, 8, 512
EPS = 1e-5


def layernorm(r, g):
    mu = r.mean(-1, keepdims=True)
    var = ((r - mu) ** 2).mean(-1, keepdims=True)
    return (r - mu) / np.sqrt(var + EPS) * g


def setup_inputs():
    t = mx_kscale(FF)
    z = np.random.standard_normal((B, T, FF))
    return {
        "y_act": bf(z * z / (1.0 + np.exp(-z)) * t),
        "h": bf(np.random.standard_normal((B, T, E))),
        "W2": bf(np.random.standard_normal((FF, E)) / np.sqrt(FF) / t[:, None]),
        "b2": bf(np.random.standard_normal(E) * 0.1),
        "g2": bf(1.0 + np.random.standard_normal(E) * 0.1),
    }


def core(y_act, h, W2, b2, g2):
    ff = (mxq(f64(y_act), 2, "e4m3") @ mxq(f64(W2), 0, "e4m3")) + f64(b2)
    return layernorm(ff + f64(h), f64(g2))


def e4m3fn_bytes(y):
    return np.clip(np.asarray(y, np.float64), -448.0, 448.0).astype(np.float32).astype(ml_dtypes.float8_e4m3fn).view(np.uint8)


Y_SCALE = 220.0


def reference(y_act, h, W2, b2, g2):
    out = core(y_act, h, W2, b2, g2)
    return out, e4m3fn_bytes(out * Y_SCALE)

@@ -1,0 +1,358 @@
+from contextlib import ExitStack
+
+import concourse.mybir as mybir
+from concourse.masks import make_identity
+
+F32 = mybir.dt.float32
+BF16 = mybir.dt.bfloat16
+U32 = mybir.dt.uint32
+U8 = mybir.dt.uint8
+FP8X4 = mybir.dt.float8_e4m3fn_x4
+FP8 = mybir.dt.float8_e4m3fn
+ALU = mybir.AluOpType
+ACT = mybir.ActivationFunctionType
+
+P = 128
+K = 512
+E = 1024
+ROWS = 4096
+HALF = 512
+NT = ROWS // P
+GROUP = 4
+NG = NT // GROUP
+EPS = 1e-5
+Y_SCALE = 220.0
+FLOPS = 2 * ROWS * K * E
+
+TYPES = ["V" if t % 4 == 0 else "G" for t in range(NT)]
+X_ON = ["G" for t in range(NT)]
+LEAD = 3
+LF = 3
+LX = 2
+LO = 2
+BATCHES = [[0], [1], [2, 3], [4, 5], [6, 7]]
+PRELOAD = 4
+QLEAD = 2
+
+
+def tile_transformerblock_pb_t_kernel(tc, y_act, h, W2, b2, g2, out_0, out_1):
+    nc = tc.nc
+    yv = y_act.flatten_outer_dims().rearrange("(g p j) k -> g p j k", p=P, j=GROUP)
+    hv = h.flatten_outer_dims().rearrange("(g p j) e -> g p j e", p=P, j=GROUP)
+    o0v = out_0.flatten_outer_dims().rearrange("(g p j) e -> g p j e", p=P, j=GROUP)
+    o1v = out_1.flatten_outer_dims().rearrange("(g p j) e -> g p (j e)", p=P, j=GROUP)
+    wv = W2.rearrange("(p j) e -> p j e", j=4)
+
+    with ExitStack() as ctx:
+        keep = ctx.enter_context(tc.tile_pool(name="keep", bufs=1))
+        yraw_pool = ctx.enter_context(tc.tile_pool(name="yraw", bufs=8))
+        hraw_pool = ctx.enter_context(tc.tile_pool(name="hraw", bufs=5))
+        ygrp_pool = ctx.enter_context(tc.tile_pool(name="ygrp", bufs=2))
+        ycode_pool = ctx.enter_context(tc.tile_pool(name="ycode", bufs=3))
+        r_pool = ctx.enter_context(tc.tile_pool(name="rp", bufs=8))
+        u_pool = ctx.enter_context(tc.tile_pool(name="up", bufs=6))
+        o8_pool = ctx.enter_context(tc.tile_pool(name="o8p", bufs=3))
+        sq_pool = ctx.enter_context(tc.tile_pool(name="sqp", bufs=2))
+        st_pool = ctx.enter_context(tc.tile_pool(name="stp", bufs=8))
+        cst_ps = ctx.enter_context(tc.psum_pool(name="cstps", bufs=1))
+        mx_ps = ctx.enter_context(tc.psum_pool(name="mxps", bufs=1))
+        tp_ps = ctx.enter_context(tc.psum_pool(name="tpps", bufs=2))
+        ctx.enter_context(tc.manual_schedule())
+
+        halves = [slice(0, HALF), slice(HALF, E)]
+
+        bg = keep.tile([P, 2 * E], BF16, name="bg", tag="bg")
+        ones = keep.tile([P, P], BF16, name="ones", tag="ones")
+        eps_t = keep.tile([P, 1], F32, name="eps_t", tag="eps_t")
+        warm = keep.tile([P, 1], F32, name="warm", tag="warm")
+        ident = keep.tile([P, P], F32, name="ident", tag="ident")
+        nc.vector.memset(bg[:], 0.0)
+        nc.vector.memset(ones[:], 1.0)
+        nc.vector.memset(eps_t[:], EPS)
+        make_identity(nc, ident[:])
+
+        nc.scalar.dma_start(out=bg[0:1, 0:E], in_=b2.rearrange("(o e) -> o e", o=1))
+        nc.scalar.dma_start(out=bg[0:1, E : 2 * E], in_=g2.rearrange("(o e) -> o e", o=1))
+        nc.scalar.activation(out=warm[:], in_=eps_t[:], func=ACT.Sqrt)
+
+        w_raw = [keep.tile([P, 4, HALF], BF16, name="w_raw%d" % c, tag="w_raw%d" % c) for c in range(2)]
+        w_grp = [
+            keep.tile([P, HALF, 4], BF16, name="w_grp%d" % c, tag="w_grp%d" % c, align_bytes=64) for c in range(2)
+        ]
+        w_codes = keep.tile([P, E], U32, name="w_codes", tag="w_codes", align_bytes=64)
+        w_scales = keep.tile([P, E], U8, name="w_scales", tag="w_scales", align_bytes=64)
+
+        y_raw = {}
+        h_raw = {}
+
+        def load_y(g):
+            y_raw[g] = yraw_pool.tile([P, GROUP, K], BF16, name="y_raw", tag="y_raw")
+            nc.sync.dma_start(out=y_raw[g][:], in_=yv[g])
+
+        def load_h(g, split):
+            h_raw[g] = hraw_pool.tile([P, GROUP, E], BF16, name="h_raw", tag="h_raw")
+            if split:
+                for j in range(GROUP):
+                    nc.sync.dma_start(out=h_raw[g][:, j, :], in_=hv[g][:, j, :])
+            else:
+                nc.sync.dma_start(out=h_raw[g][:], in_=hv[g])
+
+        nc.sync.dma_start(out=w_raw[0][:], in_=wv[:, :, halves[0]])
+        load_y(0)
+        nc.sync.dma_start(out=w_raw[1][:], in_=wv[:, :, halves[1]])
+        load_h(0, True)
+        for g in range(1, PRELOAD):
+            load_y(g)
+            load_h(g, False)
+
+        b2p = [cst_ps.tile([P, HALF], F32, name="b2p%d" % c, tag="b2p%d" % c) for c in range(2)]
+        g2p = [cst_ps.tile([P, HALF], F32, name="g2p%d" % c, tag="g2p%d" % c) for c in range(2)]
+        for c in range(2):
+            nc.tensor.matmul(out=b2p[c][:], lhsT=ones[:], rhs=bg[:, c * HALF : (c + 1) * HALF], start=True, stop=True)
+        for c in range(2):
+            nc.tensor.matmul(
+                out=g2p[c][:], lhsT=ones[:], rhs=bg[:, E + c * HALF : E + (c + 1) * HALF], start=True, stop=True
+            )
+
+        for c in range(2):
+            nc.vector.tensor_copy(out=w_grp[c][:], in_=w_raw[c][:].rearrange("p j w -> p w j"))
+            nc.vector.quantize_mx(
+                out=w_codes[:, halves[c]].bitcast(FP8X4),
+                scales=w_scales[:, halves[c]],
+                in_=w_grp[c][:].rearrange("p w j -> p (w j)"),
+            )
+
+        batch_of = {}
+        for bi, b in enumerate(BATCHES):
+            for k, g in enumerate(b):
+                batch_of[g] = (bi, k)
+        y_grp = {}
+        y_codes = {}
+        y_scales = {}
+
+        def prep_pair(g, q):
+            bi, k = batch_of[g]
+            nb = len(BATCHES[bi])
+            if bi not in y_grp:
+                y_grp[bi] = ygrp_pool.tile([P, nb * GROUP * P * 4], BF16, name="y_grp", tag="y_grp", align_bytes=64)
+            tp = tp_ps.tile([P, 2, 2, P], F32, name="tp", tag="tp")
+            for jj in range(2):
+                words = y_raw[g][:, 2 * q + jj, :].bitcast(F32)
+                for u in range(2):
+                    nc.tensor.transpose(tp[:, jj, u, :], words[:, u : K // 2 : 2], ident[:])
+            base = (k * GROUP + 2 * q) * 2 * P
+            nc.scalar.copy(
+                out=y_grp[bi][:].bitcast(F32)[:, base : base + 4 * P].rearrange("p (jj r u) -> p jj r u", jj=2, u=2),
+                in_=tp[:].rearrange("p jj u r -> p jj r u"),
+            )
+
+        def quantise_batch(bi):
+            nb = len(BATCHES[bi])
+            y_codes[bi] = ycode_pool.tile([P, nb * GROUP * P], U32, name="y_codes", tag="y_codes", align_bytes=64)
+            y_scales[bi] = ycode_pool.tile([P, nb * GROUP * P], U8, name="y_scales", tag="y_scales", align_bytes=64)
+            nc.vector.quantize_mx(out=y_codes[bi][:].bitcast(FP8X4), scales=y_scales[bi][:], in_=y_grp[bi][:])
+
+        plan = {}
+        head_prep = []
+        for bi, b in enumerate(BATCHES):
+            pairs = [(g, q) for g in b for q in range(2)]
+            qs = GROUP * b[0] - QLEAD
+            for k, pr in enumerate(pairs):
+                s = qs - (len(pairs) - k)
+                if s < 0:
+                    head_prep.append(("TC", pr[0], pr[1]))
+                else:
+                    plan.setdefault(s, []).append(("TC", pr[0], pr[1]))
+            if qs < 0:
+                head_prep.append(("Q", bi, 0))
+            else:
+                plan.setdefault(qs, []).append(("Q", bi, 0))
+
+        def do_prep(a):
+            if a[0] == "TC":
+                prep_pair(a[1], a[2])
+            else:
+                quantise_batch(a[1])
+
+        for a in head_prep:
+            do_prep(a)
+
+        b2s = keep.tile([P, E], F32, name="b2s", tag="b2s")
+        sb = keep.tile([P, 4], F32, name="sb", tag="sb")
+        for c in range(2):
+            nc.scalar.activation(out=b2s[:, halves[c]], in_=b2p[c][:], func=ACT.Copy, accum_out=sb[:, c : c + 1])
+        nb2h = keep.tile([P, 1], F32, name="nb2h", tag="nb2h")
+        nc.scalar.activation(
+            out=sb[:, 2:4], in_=sb[:, 0:2], func=ACT.Copy, scale=-1.0 / (2.0 * E), accum_out=nb2h[:, 0:1]
+        )
+
+        r_t = {}
+        u_t = {}
+        st = {}
+        mx = {}
+        o8 = {}
+
+        def stage_h(t):
+            r_t[t] = r_pool.tile([P, E], F32, name="r_t", tag="r_t")
+            nc.gpsimd.tensor_tensor(out=r_t[t][:], in0=h_raw[t // GROUP][:, t % GROUP, :], in1=b2s[:], op=ALU.add)
+
+        def stage_m(t):
+            bi, k = batch_of[t // GROUP]
+            cols = slice((k * GROUP + t % GROUP) * P, (k * GROUP + t % GROUP + 1) * P)
+            mx[t] = []
+            for c in range(2):
+                acc = mx_ps.tile([P, HALF], F32, name="mx%d" % c, tag="mx%d" % c)
+                mx[t].append(acc)
+                nc.tensor.matmul_mx(
+                    out=acc[:],
+                    lhsT=y_codes[bi][:, cols].bitcast(FP8X4),
+                    lhsT_scale=y_scales[bi][:, cols],
+                    rhs=w_codes[:, halves[c]].bitcast(FP8X4),
+                    rhs_scale=w_scales[:, halves[c]],
+                    start=True,
+                    stop=True,
+                )
+
+        def stage_p1(t):
+            if TYPES[t] == "V":
+                r_t[t] = r_pool.tile([P, E], F32, name="r_t", tag="r_t")
+            st[t] = st_pool.tile([P, 8], F32, name="st", tag="st")
+            for c in range(2):
+                if TYPES[t] == "V":
+                    other = h_raw[t // GROUP][:, t % GROUP, halves[c]]
+                else:
+                    other = r_t[t][:, halves[c]]
+                nc.vector.scalar_tensor_tensor(
+                    out=r_t[t][:, halves[c]],
+                    in0=mx[t][c][:],
+                    scalar=1.0,
+                    in1=other,
+                    op0=ALU.mult,
+                    op1=ALU.add,
+                    accum_out=st[t][:, c : c + 1],
+                )
+
+        def stage_mu(t):
+            if TYPES[t] == "V":
+                nc.scalar.activation(
+                    out=st[t][:, 6:8],
+                    in_=st[t][:, 0:2],
+                    func=ACT.Identity,
+                    scale=-1.0 / E,
+                    bias=nb2h[:, 0:1],
+                    accum_out=st[t][:, 2:3],
+                )
+            else:
+                nc.scalar.activation(
+                    out=st[t][:, 6:8], in_=st[t][:, 0:2], func=ACT.Copy, scale=-1.0 / E, accum_out=st[t][:, 2:3]
+                )
+
+        def stage_sq(t):
+            junk = sq_pool.tile([P, E], BF16, name="junk", tag="junk")
+            if TYPES[t] == "V":
+                nc.scalar.activation(out=junk[:], in_=r_t[t][:], func=ACT.Square, accum_out=st[t][:, 3:4])
+            else:
+                nc.scalar.activation(
+                    out=junk[:], in_=r_t[t][:], func=ACT.Square, bias=st[t][:, 2:3], accum_out=st[t][:, 3:4]
+                )
+            nc.scalar.activation(
+                out=st[t][:, 4:5], in_=st[t][:, 3:4], func=ACT.Sqrt, scale=1.0 / E, bias=eps_t[:, 0:1]
+            )
+
+        def stage_rc(t):
+            nc.vector.reciprocal(out=st[t][:, 5:6], in_=st[t][:, 4:5])
+
+        def stage_s2(t):
+            if TYPES[t] == "G":
+                u_t[t] = u_pool.tile([P, E], F32, name="u_t", tag="u_t")
+            for c in range(2):
+                if TYPES[t] == "G":
+                    nc.vector.scalar_tensor_tensor(
+                        out=u_t[t][:, halves[c]],
+                        in0=r_t[t][:, halves[c]],
+                        scalar=st[t][:, 2:3],
+                        in1=g2p[c][:],
+                        op0=ALU.add,
+                        op1=ALU.mult,
+                    )
+                else:
+                    nc.vector.scalar_tensor_tensor(
+                        out=r_t[t][:, halves[c]],
+                        in0=r_t[t][:, halves[c]],
+                        scalar=st[t][:, 2:3],
+                        in1=b2p[c][:],
+                        op0=ALU.add,
+                        op1=ALU.add,
+                    )
+
+        def stage_o(t):
+            u_t[t] = u_pool.tile([P, E], F32, name="u_t", tag="u_t")
+            for c in range(2):
+                nc.vector.scalar_tensor_tensor(
+                    out=u_t[t][:, halves[c]],
+                    in0=r_t[t][:, halves[c]],
+                    scalar=st[t][:, 5:6],
+                    in1=g2p[c][:],
+                    op0=ALU.mult,
+                    op1=ALU.mult,
+                )
+
+        def stage_x(t):
+            if X_ON[t] == "G":
+                nc.gpsimd.tensor_scalar(
+                    out=u_t[t][:], in0=u_t[t][:], scalar1=st[t][:, 5:6], scalar2=0.0, op0=ALU.mult, op1=ALU.add
+                )
+            else:
+                nc.scalar.activation(out=u_t[t][:], in_=u_t[t][:], func=ACT.Copy, scale=st[t][:, 5:6])
+
+        def stage_f(t):
+            g = t // GROUP
+            j = t % GROUP
+            nc.sync.dma_start(out=o0v[g][:, j, :], in_=u_t[t][:])
+            if j == 0:
+                o8[g] = o8_pool.tile([P, GROUP, E], FP8, name="o8", tag="o8")
+            nc.scalar.activation(out=o8[g][:, j, :], in_=u_t[t][:], func=ACT.Copy, scale=Y_SCALE, saturate=False)
+            if j == GROUP - 1:
+                nc.sync.dma_start(out=o1v[g], in_=o8[g][:].rearrange("p j e -> p (j e)").bitcast(U8))
+
+        g_tiles = [t for t in range(NT) if TYPES[t] == "G"]
+        h_done = [0]
+
+        def h_upto(t):
+            while h_done[0] < len(g_tiles) and g_tiles[h_done[0]] <= t:
+                stage_h(g_tiles[h_done[0]])
+                h_done[0] += 1
+
+        def ok(t):
+            return 0 <= t < NT
+
+        stage_m(0)
+        for s in range(NT + LF + 1):
+            h_upto(min(NT - 1, s + LEAD))
+            if ok(s):
+                stage_p1(s)
+                if ok(s + 1):
+                    stage_m(s + 1)
+                stage_mu(s)
+                if TYPES[s] == "G":
+                    stage_sq(s)
+            if ok(s - 1):
+                stage_s2(s - 1)
+                if TYPES[s - 1] == "V":
+                    stage_sq(s - 1)
+                else:
+                    stage_rc(s - 1)
+            if ok(s - LO) and TYPES[s - LO] == "V":
+                stage_rc(s - LO)
+                stage_o(s - LO)
+            if ok(s - LX) and TYPES[s - LX] == "G":
+                stage_x(s - LX)
+            if ok(s - LF):
+                stage_f(s - LF)
+            for a in plan.get(s, []):
+                do_prep(a)
+            if ok(s) and s % GROUP == 1:
+                gl = s // GROUP + PRELOAD
+                if gl < NG:
+                    load_y(gl)
+                    load_h(gl, False)

@@ -24,7 +24,7 @@ EPS = 1e-5
 Y_SCALE = 220.0
 FLOPS = 2 * ROWS * K * E
 
-TYPES = ["V" if t % 4 == 0 else "G" for t in range(NT)]
+TYPES = ["V" if (t % 4 == 0 or t == 1) else "G" for t in range(NT)]
 X_ON = ["G" for t in range(NT)]
 LEAD = 3
 LF = 3
@@ -73,7 +73,7 @@ def tile_transformerblock_pb_t_kernel(tc, y_act, h, W2, b2, g2, out_0, out_1):
 
         nc.scalar.dma_start(out=bg[0:1, 0:E], in_=b2.rearrange("(o e) -> o e", o=1))
         nc.scalar.dma_start(out=bg[0:1, E : 2 * E], in_=g2.rearrange("(o e) -> o e", o=1))
-        nc.scalar.activation(out=warm[:], in_=eps_t[:], func=ACT.Sqrt)
+        nc.scalar.activation(out=warm[:], in_=eps_t[:], func=ACT.Abs_reciprocal_sqrt)
 
         w_raw = [keep.tile([P, 4, HALF], BF16, name="w_raw%d" % c, tag="w_raw%d" % c) for c in range(2)]
         w_grp = [
@@ -104,15 +104,6 @@ def tile_transformerblock_pb_t_kernel(tc, y_act, h, W2, b2, g2, out_0, out_1):
         for g in range(1, PRELOAD):
             load_y(g)
             load_h(g, False)
-
-        b2p = [cst_ps.tile([P, HALF], F32, name="b2p%d" % c, tag="b2p%d" % c) for c in range(2)]
-        g2p = [cst_ps.tile([P, HALF], F32, name="g2p%d" % c, tag="g2p%d" % c) for c in range(2)]
-        for c in range(2):
-            nc.tensor.matmul(out=b2p[c][:], lhsT=ones[:], rhs=bg[:, c * HALF : (c + 1) * HALF], start=True, stop=True)
-        for c in range(2):
-            nc.tensor.matmul(
-                out=g2p[c][:], lhsT=ones[:], rhs=bg[:, E + c * HALF : E + (c + 1) * HALF], start=True, stop=True
-            )
 
         for c in range(2):
             nc.vector.tensor_copy(out=w_grp[c][:], in_=w_raw[c][:].rearrange("p j w -> p w j"))
@@ -177,6 +168,15 @@ def tile_transformerblock_pb_t_kernel(tc, y_act, h, W2, b2, g2, out_0, out_1):
         for a in head_prep:
             do_prep(a)
 
+        b2p = [cst_ps.tile([P, HALF], F32, name="b2p%d" % c, tag="b2p%d" % c) for c in range(2)]
+        g2p = [cst_ps.tile([P, HALF], F32, name="g2p%d" % c, tag="g2p%d" % c) for c in range(2)]
+        for c in range(2):
+            nc.tensor.matmul(out=b2p[c][:], lhsT=ones[:], rhs=bg[:, c * HALF : (c + 1) * HALF], start=True, stop=True)
+        for c in range(2):
+            nc.tensor.matmul(
+                out=g2p[c][:], lhsT=ones[:], rhs=bg[:, E + c * HALF : E + (c + 1) * HALF], start=True, stop=True
+            )
+
         b2s = keep.tile([P, E], F32, name="b2s", tag="b2s")
         sb = keep.tile([P, 4], F32, name="sb", tag="sb")
         for c in range(2):
@@ -224,9 +224,9 @@ def tile_transformerblock_pb_t_kernel(tc, y_act, h, W2, b2, g2, out_0, out_1):
                     other = r_t[t][:, halves[c]]
                 nc.vector.scalar_tensor_tensor(
                     out=r_t[t][:, halves[c]],
-                    in0=mx[t][c][:],
+                    in0=other,
                     scalar=1.0,
-                    in1=other,
+                    in1=mx[t][c][:],
                     op0=ALU.mult,
                     op1=ALU.add,
                     accum_out=st[t][:, c : c + 1],
@@ -255,12 +255,11 @@ def tile_transformerblock_pb_t_kernel(tc, y_act, h, W2, b2, g2, out_0, out_1):
                 nc.scalar.activation(
                     out=junk[:], in_=r_t[t][:], func=ACT.Square, bias=st[t][:, 2:3], accum_out=st[t][:, 3:4]
                 )
-            nc.scalar.activation(
-                out=st[t][:, 4:5], in_=st[t][:, 3:4], func=ACT.Sqrt, scale=1.0 / E, bias=eps_t[:, 0:1]
-            )
 
-        def stage_rc(t):
-            nc.vector.reciprocal(out=st[t][:, 5:6], in_=st[t][:, 4:5])
+        def stage_rs(t):
+            nc.scalar.activation(
+                out=st[t][:, 5:6], in_=st[t][:, 3:4], func=ACT.Abs_reciprocal_sqrt, scale=1.0 / E, bias=eps_t[:, 0:1]
+            )
 
         def stage_s2(t):
             if TYPES[t] == "G":
@@ -327,6 +326,7 @@ def tile_transformerblock_pb_t_kernel(tc, y_act, h, W2, b2, g2, out_0, out_1):
             return 0 <= t < NT
 
         stage_m(0)
+        pend = []
         for s in range(NT + LF + 1):
             h_upto(min(NT - 1, s + LEAD))
             if ok(s):
@@ -334,21 +334,23 @@ def tile_transformerblock_pb_t_kernel(tc, y_act, h, W2, b2, g2, out_0, out_1):
                 if ok(s + 1):
                     stage_m(s + 1)
                 stage_mu(s)
-                if TYPES[s] == "G":
-                    stage_sq(s)
+            for t in pend:
+                stage_rs(t)
+            pend.clear()
+            if ok(s - LF):
+                stage_f(s - LF)
             if ok(s - 1):
                 stage_s2(s - 1)
                 if TYPES[s - 1] == "V":
                     stage_sq(s - 1)
-                else:
-                    stage_rc(s - 1)
+                    pend.append(s - 1)
+            if ok(s) and TYPES[s] == "G":
+                stage_sq(s)
+                pend.append(s)
             if ok(s - LO) and TYPES[s - LO] == "V":
-                stage_rc(s - LO)
                 stage_o(s - LO)
             if ok(s - LX) and TYPES[s - LX] == "G":
                 stage_x(s - LX)
-            if ok(s - LF):
-                stage_f(s - LF)
             for a in plan.get(s, []):
                 do_prep(a)
             if ok(s) and s % GROUP == 1:

@@ -25,12 +25,14 @@ Y_SCALE = 220.0
 FLOPS = 2 * ROWS * K * E
 
 TYPES = ["V" if (t % 4 == 0 or t == 1) else "G" for t in range(NT)]
-X_ON = ["G" for t in range(NT)]
-LEAD = 3
+LEAD = 1
+H_LATE = True
 LF = 3
+LFV = 3
 LX = 2
 LO = 2
-BATCHES = [[0], [1], [2, 3], [4, 5], [6, 7]]
+TAIL = False
+BATCHES = [[0], [1], [2, 3], [4, 5, 6, 7], [8, 9, 10, 11], [12, 13, 14, 15]]
 PRELOAD = 4
 QLEAD = 2
 
@@ -40,7 +42,7 @@ def tile_transformerblock_pb_t_kernel(tc, y_act, h, W2, b2, g2, out_0, out_1):
     yv = y_act.flatten_outer_dims().rearrange("(g p j) k -> g p j k", p=P, j=GROUP)
     hv = h.flatten_outer_dims().rearrange("(g p j) e -> g p j e", p=P, j=GROUP)
     o0v = out_0.flatten_outer_dims().rearrange("(g p j) e -> g p j e", p=P, j=GROUP)
-    o1v = out_1.flatten_outer_dims().rearrange("(g p j) e -> g p (j e)", p=P, j=GROUP)
+    o1v = out_1.flatten_outer_dims().rearrange("(g p j) e -> g p j e", p=P, j=GROUP)
     wv = W2.rearrange("(p j) e -> p j e", j=4)
 
     with ExitStack() as ctx:
@@ -89,24 +91,27 @@ def tile_transformerblock_pb_t_kernel(tc, y_act, h, W2, b2, g2, out_0, out_1):
             y_raw[g] = yraw_pool.tile([P, GROUP, K], BF16, name="y_raw", tag="y_raw")
             nc.sync.dma_start(out=y_raw[g][:], in_=yv[g])
 
-        def load_h(g, split):
+        def load_h(g):
             h_raw[g] = hraw_pool.tile([P, GROUP, E], BF16, name="h_raw", tag="h_raw")
-            if split:
-                for j in range(GROUP):
-                    nc.sync.dma_start(out=h_raw[g][:, j, :], in_=hv[g][:, j, :])
-            else:
-                nc.sync.dma_start(out=h_raw[g][:], in_=hv[g])
+            nc.sync.dma_start(out=h_raw[g][:], in_=hv[g])
 
+        y_raw[0] = yraw_pool.tile([P, GROUP, K], BF16, name="y_raw", tag="y_raw")
+        h_raw[0] = hraw_pool.tile([P, GROUP, E], BF16, name="h_raw", tag="h_raw")
         nc.sync.dma_start(out=w_raw[0][:], in_=wv[:, :, halves[0]])
-        load_y(0)
+        nc.sync.dma_start(out=y_raw[0][:, 0:2, :], in_=yv[0][:, 0:2, :])
         nc.sync.dma_start(out=w_raw[1][:], in_=wv[:, :, halves[1]])
-        load_h(0, True)
+        nc.sync.dma_start(out=h_raw[0][:, 0, :], in_=hv[0][:, 0, :])
+        nc.sync.dma_start(out=y_raw[0][:, 2:4, :], in_=yv[0][:, 2:4, :])
+        for j in range(1, GROUP):
+            nc.sync.dma_start(out=h_raw[0][:, j, :], in_=hv[0][:, j, :])
         for g in range(1, PRELOAD):
             load_y(g)
-            load_h(g, False)
+            load_h(g)
 
-        for c in range(2):
+        def w_copy(c):
             nc.vector.tensor_copy(out=w_grp[c][:], in_=w_raw[c][:].rearrange("p j w -> p w j"))
+
+        def w_quant(c):
             nc.vector.quantize_mx(
                 out=w_codes[:, halves[c]].bitcast(FP8X4),
                 scales=w_scales[:, halves[c]],
@@ -115,23 +120,23 @@ def tile_transformerblock_pb_t_kernel(tc, y_act, h, W2, b2, g2, out_0, out_1):
 
         batch_of = {}
         for bi, b in enumerate(BATCHES):
-            for k, g in enumerate(b):
-                batch_of[g] = (bi, k)
+            for k, pr in enumerate(b):
+                batch_of[pr] = (bi, k)
         y_grp = {}
         y_codes = {}
         y_scales = {}
 
-        def prep_pair(g, q):
-            bi, k = batch_of[g]
+        def prep_pair(pr):
+            bi, k = batch_of[pr]
             nb = len(BATCHES[bi])
             if bi not in y_grp:
-                y_grp[bi] = ygrp_pool.tile([P, nb * GROUP * P * 4], BF16, name="y_grp", tag="y_grp", align_bytes=64)
+                y_grp[bi] = ygrp_pool.tile([P, nb * 2 * P * 4], BF16, name="y_grp", tag="y_grp", align_bytes=64)
             tp = tp_ps.tile([P, 2, 2, P], F32, name="tp", tag="tp")
             for jj in range(2):
-                words = y_raw[g][:, 2 * q + jj, :].bitcast(F32)
+                words = y_raw[pr // 2][:, 2 * (pr % 2) + jj, :].bitcast(F32)
                 for u in range(2):
                     nc.tensor.transpose(tp[:, jj, u, :], words[:, u : K // 2 : 2], ident[:])
-            base = (k * GROUP + 2 * q) * 2 * P
+            base = k * 4 * P
             nc.scalar.copy(
                 out=y_grp[bi][:].bitcast(F32)[:, base : base + 4 * P].rearrange("p (jj r u) -> p jj r u", jj=2, u=2),
                 in_=tp[:].rearrange("p jj u r -> p jj r u"),
@@ -139,34 +144,37 @@ def tile_transformerblock_pb_t_kernel(tc, y_act, h, W2, b2, g2, out_0, out_1):
 
         def quantise_batch(bi):
             nb = len(BATCHES[bi])
-            y_codes[bi] = ycode_pool.tile([P, nb * GROUP * P], U32, name="y_codes", tag="y_codes", align_bytes=64)
-            y_scales[bi] = ycode_pool.tile([P, nb * GROUP * P], U8, name="y_scales", tag="y_scales", align_bytes=64)
+            y_codes[bi] = ycode_pool.tile([P, nb * 2 * P], U32, name="y_codes", tag="y_codes", align_bytes=64)
+            y_scales[bi] = ycode_pool.tile([P, nb * 2 * P], U8, name="y_scales", tag="y_scales", align_bytes=64)
             nc.vector.quantize_mx(out=y_codes[bi][:].bitcast(FP8X4), scales=y_scales[bi][:], in_=y_grp[bi][:])
 
         plan = {}
         head_prep = []
         for bi, b in enumerate(BATCHES):
-            pairs = [(g, q) for g in b for q in range(2)]
-            qs = GROUP * b[0] - QLEAD
-            for k, pr in enumerate(pairs):
-                s = qs - (len(pairs) - k)
+            qs = 2 * b[0] - QLEAD
+            for k, pr in enumerate(b):
+                s = qs - (len(b) - k)
                 if s < 0:
-                    head_prep.append(("TC", pr[0], pr[1]))
+                    head_prep.append(("TC", pr))
                 else:
-                    plan.setdefault(s, []).append(("TC", pr[0], pr[1]))
+                    plan.setdefault(s, []).append(("TC", pr))
             if qs < 0:
-                head_prep.append(("Q", bi, 0))
+                head_prep.append(("Q", bi))
             else:
-                plan.setdefault(qs, []).append(("Q", bi, 0))
+                plan.setdefault(qs, []).append(("Q", bi))
 
         def do_prep(a):
             if a[0] == "TC":
-                prep_pair(a[1], a[2])
+                prep_pair(a[1])
             else:
                 quantise_batch(a[1])
 
+        w_copy(0)
+        w_quant(0)
+        w_copy(1)
         for a in head_prep:
             do_prep(a)
+        w_quant(1)
 
         b2p = [cst_ps.tile([P, HALF], F32, name="b2p%d" % c, tag="b2p%d" % c) for c in range(2)]
         g2p = [cst_ps.tile([P, HALF], F32, name="g2p%d" % c, tag="g2p%d" % c) for c in range(2)]
@@ -191,14 +199,15 @@ def tile_transformerblock_pb_t_kernel(tc, y_act, h, W2, b2, g2, out_0, out_1):
         st = {}
         mx = {}
         o8 = {}
+        casts = {}
 
         def stage_h(t):
             r_t[t] = r_pool.tile([P, E], F32, name="r_t", tag="r_t")
             nc.gpsimd.tensor_tensor(out=r_t[t][:], in0=h_raw[t // GROUP][:, t % GROUP, :], in1=b2s[:], op=ALU.add)
 
         def stage_m(t):
-            bi, k = batch_of[t // GROUP]
-            cols = slice((k * GROUP + t % GROUP) * P, (k * GROUP + t % GROUP + 1) * P)
+            bi, k = batch_of[t // 2]
+            cols = slice((2 * k + t % 2) * P, (2 * k + t % 2 + 1) * P)
             mx[t] = []
             for c in range(2):
                 acc = mx_ps.tile([P, HALF], F32, name="mx%d" % c, tag="mx%d" % c)
@@ -284,6 +293,9 @@ def tile_transformerblock_pb_t_kernel(tc, y_act, h, W2, b2, g2, out_0, out_1):
                         op1=ALU.add,
                     )
 
+        def store_0(t):
+            nc.sync.dma_start(out=o0v[t // GROUP][:, t % GROUP, :], in_=u_t[t][:])
+
         def stage_o(t):
             u_t[t] = u_pool.tile([P, E], F32, name="u_t", tag="u_t")
             for c in range(2):
@@ -295,24 +307,35 @@ def tile_transformerblock_pb_t_kernel(tc, y_act, h, W2, b2, g2, out_0, out_1):
                     op0=ALU.mult,
                     op1=ALU.mult,
                 )
+            store_0(t)
 
         def stage_x(t):
-            if X_ON[t] == "G":
-                nc.gpsimd.tensor_scalar(
-                    out=u_t[t][:], in0=u_t[t][:], scalar1=st[t][:, 5:6], scalar2=0.0, op0=ALU.mult, op1=ALU.add
+            nc.gpsimd.tensor_scalar(
+                out=u_t[t][:], in0=u_t[t][:], scalar1=st[t][:, 5:6], scalar2=0.0, op0=ALU.mult, op1=ALU.add
+            )
+            store_0(t)
+
+        def o8_of(g):
+            if g not in o8:
+                o8[g] = o8_pool.tile([P, GROUP, E], FP8, name="o8", tag="o8")
+                casts[g] = 0
+            return o8[g]
+
+        def store_1(t):
+            g = t // GROUP
+            casts[g] += 1
+            if TAIL and g == NG - 1:
+                nc.sync.dma_start(out=o1v[g][:, t % GROUP, :], in_=o8[g][:, t % GROUP, :].bitcast(U8))
+            elif casts[g] == GROUP:
+                nc.sync.dma_start(
+                    out=o1v[g].rearrange("p j e -> p (j e)"), in_=o8[g][:].rearrange("p j e -> p (j e)").bitcast(U8)
                 )
-            else:
-                nc.scalar.activation(out=u_t[t][:], in_=u_t[t][:], func=ACT.Copy, scale=st[t][:, 5:6])
 
         def stage_f(t):
-            g = t // GROUP
-            j = t % GROUP
-            nc.sync.dma_start(out=o0v[g][:, j, :], in_=u_t[t][:])
-            if j == 0:
-                o8[g] = o8_pool.tile([P, GROUP, E], FP8, name="o8", tag="o8")
-            nc.scalar.activation(out=o8[g][:, j, :], in_=u_t[t][:], func=ACT.Copy, scale=Y_SCALE, saturate=False)
-            if j == GROUP - 1:
-                nc.sync.dma_start(out=o1v[g], in_=o8[g][:].rearrange("p j e -> p (j e)").bitcast(U8))
+            nc.scalar.activation(
+                out=o8_of(t // GROUP)[:, t % GROUP, :], in_=u_t[t][:], func=ACT.Copy, scale=Y_SCALE, saturate=False
+            )
+            store_1(t)
 
         g_tiles = [t for t in range(NT) if TYPES[t] == "G"]
         h_done = [0]
@@ -327,8 +350,9 @@ def tile_transformerblock_pb_t_kernel(tc, y_act, h, W2, b2, g2, out_0, out_1):
 
         stage_m(0)
         pend = []
-        for s in range(NT + LF + 1):
-            h_upto(min(NT - 1, s + LEAD))
+        for s in range(NT + max(LF, LFV) + 1):
+            if s == 0 or not H_LATE:
+                h_upto(min(NT - 1, s + LEAD))
             if ok(s):
                 stage_p1(s)
                 if ok(s + 1):
@@ -337,7 +361,9 @@ def tile_transformerblock_pb_t_kernel(tc, y_act, h, W2, b2, g2, out_0, out_1):
             for t in pend:
                 stage_rs(t)
             pend.clear()
-            if ok(s - LF):
+            if ok(s - LFV) and TYPES[s - LFV] == "V":
+                stage_f(s - LFV)
+            if ok(s - LF) and TYPES[s - LF] == "G":
                 stage_f(s - LF)
             if ok(s - 1):
                 stage_s2(s - 1)
@@ -351,10 +377,12 @@ def tile_transformerblock_pb_t_kernel(tc, y_act, h, W2, b2, g2, out_0, out_1):
                 stage_o(s - LO)
             if ok(s - LX) and TYPES[s - LX] == "G":
                 stage_x(s - LX)
+            if H_LATE:
+                h_upto(min(NT - 1, s + 1 + LEAD))
             for a in plan.get(s, []):
                 do_prep(a)
             if ok(s) and s % GROUP == 1:
                 gl = s // GROUP + PRELOAD
                 if gl < NG:
                     load_y(gl)
-                    load_h(gl, False)
+                    load_h(gl)

@@ -24,14 +24,14 @@ EPS = 1e-5
 Y_SCALE = 220.0
 FLOPS = 2 * ROWS * K * E
 
-TYPES = ["V" if (t % 4 == 0 or t == 1) else "G" for t in range(NT)]
-LEAD = 1
+TYPES = ["V" if (t < 4 or t % 8 in (1, 2)) else "G" for t in range(NT)]
+LEAD = 2
 H_LATE = True
 LF = 3
 LFV = 3
 LX = 2
 LO = 2
-TAIL = False
+TAIL = True
 BATCHES = [[0], [1], [2, 3], [4, 5, 6, 7], [8, 9, 10, 11], [12, 13, 14, 15]]
 PRELOAD = 4
 QLEAD = 2
@@ -361,6 +361,8 @@ def tile_transformerblock_pb_t_kernel(tc, y_act, h, W2, b2, g2, out_0, out_1):
             for t in pend:
                 stage_rs(t)
             pend.clear()
+            if ok(s - LX) and TYPES[s - LX] == "G":
+                stage_x(s - LX)
             if ok(s - LFV) and TYPES[s - LFV] == "V":
                 stage_f(s - LFV)
             if ok(s - LF) and TYPES[s - LF] == "G":
@@ -375,8 +377,6 @@ def tile_transformerblock_pb_t_kernel(tc, y_act, h, W2, b2, g2, out_0, out_1):
                 pend.append(s)
             if ok(s - LO) and TYPES[s - LO] == "V":
                 stage_o(s - LO)
-            if ok(s - LX) and TYPES[s - LX] == "G":
-                stage_x(s - LX)
             if H_LATE:
                 h_upto(min(NT - 1, s + 1 + LEAD))
             for a in plan.get(s, []):

@@ -24,14 +24,14 @@ EPS = 1e-5
 Y_SCALE = 220.0
 FLOPS = 2 * ROWS * K * E
 
-TYPES = ["V" if (t < 4 or t % 8 in (1, 2)) else "G" for t in range(NT)]
-LEAD = 2
+TYPES = ["V" if (t % 4 == 0 or t == 1) else "G" for t in range(NT)]
+LEAD = 1
 H_LATE = True
 LF = 3
 LFV = 3
 LX = 2
 LO = 2
-TAIL = True
+TAIL = False
 BATCHES = [[0], [1], [2, 3], [4, 5, 6, 7], [8, 9, 10, 11], [12, 13, 14, 15]]
 PRELOAD = 4
 QLEAD = 2
@@ -98,11 +98,9 @@ def tile_transformerblock_pb_t_kernel(tc, y_act, h, W2, b2, g2, out_0, out_1):
         y_raw[0] = yraw_pool.tile([P, GROUP, K], BF16, name="y_raw", tag="y_raw")
         h_raw[0] = hraw_pool.tile([P, GROUP, E], BF16, name="h_raw", tag="h_raw")
         nc.sync.dma_start(out=w_raw[0][:], in_=wv[:, :, halves[0]])
-        nc.sync.dma_start(out=y_raw[0][:, 0:2, :], in_=yv[0][:, 0:2, :])
+        nc.sync.dma_start(out=y_raw[0][:], in_=yv[0])
         nc.sync.dma_start(out=w_raw[1][:], in_=wv[:, :, halves[1]])
-        nc.sync.dma_start(out=h_raw[0][:, 0, :], in_=hv[0][:, 0, :])
-        nc.sync.dma_start(out=y_raw[0][:, 2:4, :], in_=yv[0][:, 2:4, :])
-        for j in range(1, GROUP):
+        for j in range(GROUP):
             nc.sync.dma_start(out=h_raw[0][:, j, :], in_=hv[0][:, j, :])
         for g in range(1, PRELOAD):
             load_y(g)
@@ -172,7 +170,7 @@ def tile_transformerblock_pb_t_kernel(tc, y_act, h, W2, b2, g2, out_0, out_1):
         w_copy(0)
         w_quant(0)
         w_copy(1)
-        for a in head_prep:
+        for a in head_prep[:2]:
             do_prep(a)
         w_quant(1)
 
@@ -180,10 +178,6 @@ def tile_transformerblock_pb_t_kernel(tc, y_act, h, W2, b2, g2, out_0, out_1):
         g2p = [cst_ps.tile([P, HALF], F32, name="g2p%d" % c, tag="g2p%d" % c) for c in range(2)]
         for c in range(2):
             nc.tensor.matmul(out=b2p[c][:], lhsT=ones[:], rhs=bg[:, c * HALF : (c + 1) * HALF], start=True, stop=True)
-        for c in range(2):
-            nc.tensor.matmul(
-                out=g2p[c][:], lhsT=ones[:], rhs=bg[:, E + c * HALF : E + (c + 1) * HALF], start=True, stop=True
-            )
 
         b2s = keep.tile([P, E], F32, name="b2s", tag="b2s")
         sb = keep.tile([P, 4], F32, name="sb", tag="sb")
@@ -193,6 +187,8 @@ def tile_transformerblock_pb_t_kernel(tc, y_act, h, W2, b2, g2, out_0, out_1):
         nc.scalar.activation(
             out=sb[:, 2:4], in_=sb[:, 0:2], func=ACT.Copy, scale=-1.0 / (2.0 * E), accum_out=nb2h[:, 0:1]
         )
+        for a in head_prep[2:]:
+            do_prep(a)
 
         r_t = {}
         u_t = {}
@@ -349,6 +345,10 @@ def tile_transformerblock_pb_t_kernel(tc, y_act, h, W2, b2, g2, out_0, out_1):
             return 0 <= t < NT
 
         stage_m(0)
+        for c in range(2):
+            nc.tensor.matmul(
+                out=g2p[c][:], lhsT=ones[:], rhs=bg[:, E + c * HALF : E + (c + 1) * HALF], start=True, stop=True
+            )
         pend = []
         for s in range(NT + max(LF, LFV) + 1):
             if s == 0 or not H_LATE:
@@ -361,8 +361,6 @@ def tile_transformerblock_pb_t_kernel(tc, y_act, h, W2, b2, g2, out_0, out_1):
             for t in pend:
                 stage_rs(t)
             pend.clear()
-            if ok(s - LX) and TYPES[s - LX] == "G":
-                stage_x(s - LX)
             if ok(s - LFV) and TYPES[s - LFV] == "V":
                 stage_f(s - LFV)
             if ok(s - LF) and TYPES[s - LF] == "G":
@@ -377,6 +375,8 @@ def tile_transformerblock_pb_t_kernel(tc, y_act, h, W2, b2, g2, out_0, out_1):
                 pend.append(s)
             if ok(s - LO) and TYPES[s - LO] == "V":
                 stage_o(s - LO)
+            if ok(s - LX) and TYPES[s - LX] == "G":
+                stage_x(s - LX)
             if H_LATE:
                 h_upto(min(NT - 1, s + 1 + LEAD))
             for a in plan.get(s, []):

@@ -24,14 +24,19 @@ EPS = 1e-5
 Y_SCALE = 220.0
 FLOPS = 2 * ROWS * K * E
 
-TYPES = ["V" if (t % 4 == 0 or t == 1) else "G" for t in range(NT)]
-LEAD = 1
-H_LATE = True
-LF = 3
-LFV = 3
-LX = 2
-LO = 2
-TAIL = False
+GMOD = 7
+GRES = (2, 4, 6)
+GMIN = 2
+GMAX = 30
+TYPES = ["G" if (t % GMOD in GRES and GMIN <= t <= GMAX) else "V" for t in range(NT)]
+LEAD = 2
+LFV = 5
+LFG = 5
+LN = 2
+LO = 4
+LS = 1
+RB = 10
+UB = 9
 BATCHES = [[0], [1], [2, 3], [4, 5, 6, 7], [8, 9, 10, 11], [12, 13, 14, 15]]
 PRELOAD = 4
 QLEAD = 2
@@ -51,8 +56,8 @@ def tile_transformerblock_pb_t_kernel(tc, y_act, h, W2, b2, g2, out_0, out_1):
         hraw_pool = ctx.enter_context(tc.tile_pool(name="hraw", bufs=5))
         ygrp_pool = ctx.enter_context(tc.tile_pool(name="ygrp", bufs=2))
         ycode_pool = ctx.enter_context(tc.tile_pool(name="ycode", bufs=3))
-        r_pool = ctx.enter_context(tc.tile_pool(name="rp", bufs=8))
-        u_pool = ctx.enter_context(tc.tile_pool(name="up", bufs=6))
+        r_pool = ctx.enter_context(tc.tile_pool(name="rp", bufs=RB))
+        u_pool = ctx.enter_context(tc.tile_pool(name="up", bufs=UB))
         o8_pool = ctx.enter_context(tc.tile_pool(name="o8p", bufs=3))
         sq_pool = ctx.enter_context(tc.tile_pool(name="sqp", bufs=2))
         st_pool = ctx.enter_context(tc.tile_pool(name="stp", bufs=8))
@@ -196,6 +201,7 @@ def tile_transformerblock_pb_t_kernel(tc, y_act, h, W2, b2, g2, out_0, out_1):
         mx = {}
         o8 = {}
         casts = {}
+        g2s = keep.tile([P, E], F32, name="g2s", tag="g2s")
 
         def stage_h(t):
             r_t[t] = r_pool.tile([P, E], F32, name="r_t", tag="r_t")
@@ -267,27 +273,15 @@ def tile_transformerblock_pb_t_kernel(tc, y_act, h, W2, b2, g2, out_0, out_1):
             )
 
         def stage_s2(t):
-            if TYPES[t] == "G":
-                u_t[t] = u_pool.tile([P, E], F32, name="u_t", tag="u_t")
             for c in range(2):
-                if TYPES[t] == "G":
-                    nc.vector.scalar_tensor_tensor(
-                        out=u_t[t][:, halves[c]],
-                        in0=r_t[t][:, halves[c]],
-                        scalar=st[t][:, 2:3],
-                        in1=g2p[c][:],
-                        op0=ALU.add,
-                        op1=ALU.mult,
-                    )
-                else:
-                    nc.vector.scalar_tensor_tensor(
-                        out=r_t[t][:, halves[c]],
-                        in0=r_t[t][:, halves[c]],
-                        scalar=st[t][:, 2:3],
-                        in1=b2p[c][:],
-                        op0=ALU.add,
-                        op1=ALU.add,
-                    )
+                nc.vector.scalar_tensor_tensor(
+                    out=r_t[t][:, halves[c]],
+                    in0=r_t[t][:, halves[c]],
+                    scalar=st[t][:, 2:3],
+                    in1=b2p[c][:],
+                    op0=ALU.add,
+                    op1=ALU.add,
+                )
 
         def store_0(t):
             nc.sync.dma_start(out=o0v[t // GROUP][:, t % GROUP, :], in_=u_t[t][:])
@@ -305,33 +299,27 @@ def tile_transformerblock_pb_t_kernel(tc, y_act, h, W2, b2, g2, out_0, out_1):
                 )
             store_0(t)
 
-        def stage_x(t):
+        def stage_n(t):
             nc.gpsimd.tensor_scalar(
-                out=u_t[t][:], in0=u_t[t][:], scalar1=st[t][:, 5:6], scalar2=0.0, op0=ALU.mult, op1=ALU.add
+                out=r_t[t][:], in0=r_t[t][:], scalar1=st[t][:, 2:3], scalar2=st[t][:, 5:6], op0=ALU.add, op1=ALU.mult
             )
+
+        def stage_w(t):
+            u_t[t] = u_pool.tile([P, E], F32, name="u_t", tag="u_t")
+            nc.gpsimd.tensor_tensor(out=u_t[t][:], in0=r_t[t][:], in1=g2s[:], op=ALU.mult)
             store_0(t)
 
-        def o8_of(g):
+        def stage_f(t):
+            g = t // GROUP
             if g not in o8:
                 o8[g] = o8_pool.tile([P, GROUP, E], FP8, name="o8", tag="o8")
                 casts[g] = 0
-            return o8[g]
-
-        def store_1(t):
-            g = t // GROUP
+            nc.scalar.activation(out=o8[g][:, t % GROUP, :], in_=u_t[t][:], func=ACT.Copy, scale=Y_SCALE, saturate=False)
             casts[g] += 1
-            if TAIL and g == NG - 1:
-                nc.sync.dma_start(out=o1v[g][:, t % GROUP, :], in_=o8[g][:, t % GROUP, :].bitcast(U8))
-            elif casts[g] == GROUP:
+            if casts[g] == GROUP:
                 nc.sync.dma_start(
                     out=o1v[g].rearrange("p j e -> p (j e)"), in_=o8[g][:].rearrange("p j e -> p (j e)").bitcast(U8)
                 )
-
-        def stage_f(t):
-            nc.scalar.activation(
-                out=o8_of(t // GROUP)[:, t % GROUP, :], in_=u_t[t][:], func=ACT.Copy, scale=Y_SCALE, saturate=False
-            )
-            store_1(t)
 
         g_tiles = [t for t in range(NT) if TYPES[t] == "G"]
         h_done = [0]
@@ -341,47 +329,48 @@ def tile_transformerblock_pb_t_kernel(tc, y_act, h, W2, b2, g2, out_0, out_1):
                 stage_h(g_tiles[h_done[0]])
                 h_done[0] += 1
 
-        def ok(t):
-            return 0 <= t < NT
+        def is_type(t, kind):
+            return 0 <= t < NT and TYPES[t] == kind
 
         stage_m(0)
         for c in range(2):
             nc.tensor.matmul(
                 out=g2p[c][:], lhsT=ones[:], rhs=bg[:, E + c * HALF : E + (c + 1) * HALF], start=True, stop=True
             )
+        for c in range(2):
+            nc.scalar.copy(out=g2s[:, halves[c]], in_=g2p[c][:])
         pend = []
-        for s in range(NT + max(LF, LFV) + 1):
-            if s == 0 or not H_LATE:
-                h_upto(min(NT - 1, s + LEAD))
-            if ok(s):
+        for s in range(NT + max(LFG, LFV) + 1):
+            if s == 0:
+                h_upto(LEAD)
+            if s < NT:
                 stage_p1(s)
-                if ok(s + 1):
+                if s + 1 < NT:
                     stage_m(s + 1)
                 stage_mu(s)
             for t in pend:
                 stage_rs(t)
             pend.clear()
-            if ok(s - LFV) and TYPES[s - LFV] == "V":
+            if is_type(s - LFV, "V"):
                 stage_f(s - LFV)
-            if ok(s - LF) and TYPES[s - LF] == "G":
-                stage_f(s - LF)
-            if ok(s - 1):
-                stage_s2(s - 1)
-                if TYPES[s - 1] == "V":
-                    stage_sq(s - 1)
-                    pend.append(s - 1)
-            if ok(s) and TYPES[s] == "G":
+            if is_type(s - LFG, "G"):
+                stage_f(s - LFG)
+            if is_type(s - LS, "V"):
+                stage_s2(s - LS)
+                stage_sq(s - LS)
+                pend.append(s - LS)
+            if is_type(s, "G"):
                 stage_sq(s)
                 pend.append(s)
-            if ok(s - LO) and TYPES[s - LO] == "V":
+            if is_type(s - LO, "V"):
                 stage_o(s - LO)
-            if ok(s - LX) and TYPES[s - LX] == "G":
-                stage_x(s - LX)
-            if H_LATE:
-                h_upto(min(NT - 1, s + 1 + LEAD))
+            if is_type(s - LN, "G"):
+                stage_n(s - LN)
+                stage_w(s - LN)
+            h_upto(min(NT - 1, s + 1 + LEAD))
             for a in plan.get(s, []):
                 do_prep(a)
-            if ok(s) and s % GROUP == 1:
+            if s < NT and s % GROUP == 1:
                 gl = s // GROUP + PRELOAD
                 if gl < NG:
                     load_y(gl)

@@ -24,12 +24,12 @@ EPS = 1e-5
 Y_SCALE = 220.0
 FLOPS = 2 * ROWS * K * E
 
-GMOD = 7
-GRES = (2, 4, 6)
+GMOD = 9
+GRES = (2, 4, 6, 8)
 GMIN = 2
-GMAX = 30
+GMAX = 29
 TYPES = ["G" if (t % GMOD in GRES and GMIN <= t <= GMAX) else "V" for t in range(NT)]
-LEAD = 2
+LEAD = 3
 LFV = 5
 LFG = 5
 LN = 2
@@ -40,6 +40,12 @@ UB = 9
 BATCHES = [[0], [1], [2, 3], [4, 5, 6, 7], [8, 9, 10, 11], [12, 13, 14, 15]]
 PRELOAD = 4
 QLEAD = 2
+QG = False
+ML = 1
+CL = 1
+TLAG = 0
+VCAST = (31,)
+LVC = 1
 
 
 def tile_transformerblock_pb_t_kernel(tc, y_act, h, W2, b2, g2, out_0, out_1):
@@ -62,7 +68,7 @@ def tile_transformerblock_pb_t_kernel(tc, y_act, h, W2, b2, g2, out_0, out_1):
         sq_pool = ctx.enter_context(tc.tile_pool(name="sqp", bufs=2))
         st_pool = ctx.enter_context(tc.tile_pool(name="stp", bufs=8))
         cst_ps = ctx.enter_context(tc.psum_pool(name="cstps", bufs=1))
-        mx_ps = ctx.enter_context(tc.psum_pool(name="mxps", bufs=1))
+        mx_ps = ctx.enter_context(tc.psum_pool(name="mxps", bufs=2))
         tp_ps = ctx.enter_context(tc.psum_pool(name="tpps", bufs=2))
         ctx.enter_context(tc.manual_schedule())
 
@@ -128,6 +134,7 @@ def tile_transformerblock_pb_t_kernel(tc, y_act, h, W2, b2, g2, out_0, out_1):
         y_grp = {}
         y_codes = {}
         y_scales = {}
+        tps = {}
 
         def prep_pair(pr):
             bi, k = batch_of[pr]
@@ -135,10 +142,15 @@ def tile_transformerblock_pb_t_kernel(tc, y_act, h, W2, b2, g2, out_0, out_1):
             if bi not in y_grp:
                 y_grp[bi] = ygrp_pool.tile([P, nb * 2 * P * 4], BF16, name="y_grp", tag="y_grp", align_bytes=64)
             tp = tp_ps.tile([P, 2, 2, P], F32, name="tp", tag="tp")
+            tps[pr] = tp
             for jj in range(2):
                 words = y_raw[pr // 2][:, 2 * (pr % 2) + jj, :].bitcast(F32)
                 for u in range(2):
                     nc.tensor.transpose(tp[:, jj, u, :], words[:, u : K // 2 : 2], ident[:])
+
+        def copy_pair(pr):
+            bi, k = batch_of[pr]
+            tp = tps[pr]
             base = k * 4 * P
             nc.scalar.copy(
                 out=y_grp[bi][:].bitcast(F32)[:, base : base + 4 * P].rearrange("p (jj r u) -> p jj r u", jj=2, u=2),
@@ -152,47 +164,53 @@ def tile_transformerblock_pb_t_kernel(tc, y_act, h, W2, b2, g2, out_0, out_1):
             nc.vector.quantize_mx(out=y_codes[bi][:].bitcast(FP8X4), scales=y_scales[bi][:], in_=y_grp[bi][:])
 
         plan = {}
+        q_at = {}
         head_prep = []
         for bi, b in enumerate(BATCHES):
             qs = 2 * b[0] - QLEAD
+            if bi >= 2 and QG:
+                qs = max([t for t in range(qs + 1) if TYPES[t] == "G"] + [0])
             for k, pr in enumerate(b):
-                s = qs - (len(b) - k)
-                if s < 0:
-                    head_prep.append(("TC", pr))
+                sc = qs - CL - (len(b) - 1 - k)
+                if bi < 2:
+                    head_prep.append(("T", pr))
+                    head_prep.append(("C", pr))
                 else:
-                    plan.setdefault(s, []).append(("TC", pr))
+                    plan.setdefault(max(sc - TLAG, -1), []).append(("T", pr))
+                    plan.setdefault(max(sc, -1), []).append(("C", pr))
             if qs < 0:
                 head_prep.append(("Q", bi))
-            else:
+            elif bi < 2 or not QG:
                 plan.setdefault(qs, []).append(("Q", bi))
+            else:
+                q_at[qs] = bi
 
         def do_prep(a):
-            if a[0] == "TC":
+            if a[0] == "T":
                 prep_pair(a[1])
+            elif a[0] == "C":
+                copy_pair(a[1])
             else:
                 quantise_batch(a[1])
 
         w_copy(0)
         w_quant(0)
         w_copy(1)
-        for a in head_prep[:2]:
+        for a in head_prep[:3]:
             do_prep(a)
         w_quant(1)
 
-        b2p = [cst_ps.tile([P, HALF], F32, name="b2p%d" % c, tag="b2p%d" % c) for c in range(2)]
-        g2p = [cst_ps.tile([P, HALF], F32, name="g2p%d" % c, tag="g2p%d" % c) for c in range(2)]
+        b2p = cst_ps.tile([P, E], BF16, name="b2p", tag="b2p")
+        g2p = cst_ps.tile([P, E], BF16, name="g2p", tag="g2p")
         for c in range(2):
-            nc.tensor.matmul(out=b2p[c][:], lhsT=ones[:], rhs=bg[:, c * HALF : (c + 1) * HALF], start=True, stop=True)
+            nc.tensor.matmul(out=b2p[:, halves[c]], lhsT=ones[:], rhs=bg[:, c * HALF : (c + 1) * HALF], start=True, stop=True)
 
         b2s = keep.tile([P, E], F32, name="b2s", tag="b2s")
         sb = keep.tile([P, 4], F32, name="sb", tag="sb")
-        for c in range(2):
-            nc.scalar.activation(out=b2s[:, halves[c]], in_=b2p[c][:], func=ACT.Copy, accum_out=sb[:, c : c + 1])
+        nc.scalar.activation(out=b2s[:], in_=b2p[:], func=ACT.Copy, accum_out=sb[:, 0:1])
         nb2h = keep.tile([P, 1], F32, name="nb2h", tag="nb2h")
-        nc.scalar.activation(
-            out=sb[:, 2:4], in_=sb[:, 0:2], func=ACT.Copy, scale=-1.0 / (2.0 * E), accum_out=nb2h[:, 0:1]
-        )
-        for a in head_prep[2:]:
+        nc.scalar.activation(out=nb2h[:, 0:1], in_=sb[:, 0:1], func=ACT.Copy, scale=-1.0 / (2.0 * E))
+        for a in head_prep[3:] + plan.get(-1, []):
             do_prep(a)
 
         r_t = {}
@@ -201,6 +219,7 @@ def tile_transformerblock_pb_t_kernel(tc, y_act, h, W2, b2, g2, out_0, out_1):
         mx = {}
         o8 = {}
         casts = {}
+        s1_wait = []
         g2s = keep.tile([P, E], F32, name="g2s", tag="g2s")
 
         def stage_h(t):
@@ -273,30 +292,18 @@ def tile_transformerblock_pb_t_kernel(tc, y_act, h, W2, b2, g2, out_0, out_1):
             )
 
         def stage_s2(t):
-            for c in range(2):
-                nc.vector.scalar_tensor_tensor(
-                    out=r_t[t][:, halves[c]],
-                    in0=r_t[t][:, halves[c]],
-                    scalar=st[t][:, 2:3],
-                    in1=b2p[c][:],
-                    op0=ALU.add,
-                    op1=ALU.add,
-                )
+            nc.vector.scalar_tensor_tensor(
+                out=r_t[t][:], in0=r_t[t][:], scalar=st[t][:, 2:3], in1=b2p[:], op0=ALU.add, op1=ALU.add
+            )
 
         def store_0(t):
             nc.sync.dma_start(out=o0v[t // GROUP][:, t % GROUP, :], in_=u_t[t][:])
 
         def stage_o(t):
             u_t[t] = u_pool.tile([P, E], F32, name="u_t", tag="u_t")
-            for c in range(2):
-                nc.vector.scalar_tensor_tensor(
-                    out=u_t[t][:, halves[c]],
-                    in0=r_t[t][:, halves[c]],
-                    scalar=st[t][:, 5:6],
-                    in1=g2p[c][:],
-                    op0=ALU.mult,
-                    op1=ALU.mult,
-                )
+            nc.vector.scalar_tensor_tensor(
+                out=u_t[t][:], in0=r_t[t][:], scalar=st[t][:, 5:6], in1=g2p[:], op0=ALU.mult, op1=ALU.mult
+            )
             store_0(t)
 
         def stage_n(t):
@@ -314,9 +321,23 @@ def tile_transformerblock_pb_t_kernel(tc, y_act, h, W2, b2, g2, out_0, out_1):
             if g not in o8:
                 o8[g] = o8_pool.tile([P, GROUP, E], FP8, name="o8", tag="o8")
                 casts[g] = 0
-            nc.scalar.activation(out=o8[g][:, t % GROUP, :], in_=u_t[t][:], func=ACT.Copy, scale=Y_SCALE, saturate=False)
+            if t in VCAST:
+                nc.vector.tensor_scalar(
+                    out=o8[g][:, t % GROUP, :], in0=u_t[t][:], scalar1=Y_SCALE, scalar2=None, op0=ALU.mult, saturate=False
+                )
+            else:
+                nc.scalar.activation(
+                    out=o8[g][:, t % GROUP, :], in_=u_t[t][:], func=ACT.Copy, scale=Y_SCALE, saturate=False
+                )
             casts[g] += 1
-            if casts[g] == GROUP:
+            if g == NG - 1 or casts[g] == GROUP:
+                s1_wait.append(t)
+
+        def store_1(t):
+            g = t // GROUP
+            if g == NG - 1:
+                nc.sync.dma_start(out=o1v[g][:, t % GROUP, :], in_=o8[g][:, t % GROUP, :].bitcast(U8))
+            else:
                 nc.sync.dma_start(
                     out=o1v[g].rearrange("p j e -> p (j e)"), in_=o8[g][:].rearrange("p j e -> p (j e)").bitcast(U8)
                 )
@@ -335,23 +356,26 @@ def tile_transformerblock_pb_t_kernel(tc, y_act, h, W2, b2, g2, out_0, out_1):
         stage_m(0)
         for c in range(2):
             nc.tensor.matmul(
-                out=g2p[c][:], lhsT=ones[:], rhs=bg[:, E + c * HALF : E + (c + 1) * HALF], start=True, stop=True
+                out=g2p[:, halves[c]], lhsT=ones[:], rhs=bg[:, E + c * HALF : E + (c + 1) * HALF], start=True, stop=True
             )
-        for c in range(2):
-            nc.scalar.copy(out=g2s[:, halves[c]], in_=g2p[c][:])
+        nc.scalar.copy(out=g2s[:], in_=g2p[:])
+        for t in range(1, ML):
+            stage_m(t)
         pend = []
         for s in range(NT + max(LFG, LFV) + 1):
             if s == 0:
                 h_upto(LEAD)
             if s < NT:
                 stage_p1(s)
-                if s + 1 < NT:
-                    stage_m(s + 1)
+                if s in q_at:
+                    quantise_batch(q_at[s])
+                if s + ML < NT:
+                    stage_m(s + ML)
                 stage_mu(s)
             for t in pend:
                 stage_rs(t)
             pend.clear()
-            if is_type(s - LFV, "V"):
+            if is_type(s - LFV, "V") and s - LFV not in VCAST:
                 stage_f(s - LFV)
             if is_type(s - LFG, "G"):
                 stage_f(s - LFG)
@@ -364,9 +388,14 @@ def tile_transformerblock_pb_t_kernel(tc, y_act, h, W2, b2, g2, out_0, out_1):
                 pend.append(s)
             if is_type(s - LO, "V"):
                 stage_o(s - LO)
+            if s - LO - LVC in VCAST:
+                stage_f(s - LO - LVC)
             if is_type(s - LN, "G"):
                 stage_n(s - LN)
                 stage_w(s - LN)
+            for t in s1_wait:
+                store_1(t)
+            s1_wait.clear()
             h_upto(min(NT - 1, s + 1 + LEAD))
             for a in plan.get(s, []):
                 do_prep(a)

@@ -33,17 +33,26 @@ LEAD = 3
 LFV = 5
 LFG = 5
 LN = 2
+LSG = 0
 LO = 4
+TILE_STORES_FROM = 7
 LS = 1
 RB = 10
 UB = 9
-BATCHES = [[0], [1], [2, 3], [4, 5, 6, 7], [8, 9, 10, 11], [12, 13, 14, 15]]
+BATCHES = [[0, 1], [2, 3], [4, 5, 6, 7], [8, 9, 10, 11], [12, 13, 14, 15]]
 PRELOAD = 4
 QLEAD = 2
 QG = False
 ML = 1
 CL = 1
 TLAG = 0
+QSTEP = {1: 2, 2: 6, 3: 14, 4: 22}
+TFIRST = {1: 0, 2: 2, 3: 10, 4: 18}
+TPER = {1: 1, 2: 1, 3: 1, 4: 1}
+NHEAD = 1
+HSPLIT = 5
+LOADS = [("y", 1), ("h", 1), ("y", 2), ("h", 2), ("y", 3), ("h", 3)]
+LATER = {1: [("y", 4), ("h", 4)], 5: [("y", 5), ("h", 5)], 9: [("y", 6), ("h", 6)], 13: [("y", 7), ("h", 7)]}
 VCAST = (31,)
 LVC = 1
 
@@ -113,9 +122,11 @@ def tile_transformerblock_pb_t_kernel(tc, y_act, h, W2, b2, g2, out_0, out_1):
         nc.sync.dma_start(out=w_raw[1][:], in_=wv[:, :, halves[1]])
         for j in range(GROUP):
             nc.sync.dma_start(out=h_raw[0][:, j, :], in_=hv[0][:, j, :])
-        for g in range(1, PRELOAD):
-            load_y(g)
-            load_h(g)
+        for kind, g in LOADS:
+            if kind == "y":
+                load_y(g)
+            else:
+                load_h(g)
 
         def w_copy(c):
             nc.vector.tensor_copy(out=w_grp[c][:], in_=w_raw[c][:].rearrange("p j w -> p w j"))
@@ -167,12 +178,10 @@ def tile_transformerblock_pb_t_kernel(tc, y_act, h, W2, b2, g2, out_0, out_1):
         q_at = {}
         head_prep = []
         for bi, b in enumerate(BATCHES):
-            qs = 2 * b[0] - QLEAD
-            if bi >= 2 and QG:
-                qs = max([t for t in range(qs + 1) if TYPES[t] == "G"] + [0])
+            qs = QSTEP.get(bi, -1)
             for k, pr in enumerate(b):
-                sc = qs - CL - (len(b) - 1 - k)
-                if bi < 2:
+                sc = TFIRST.get(bi, 0) + k // TPER.get(bi, 1)
+                if bi < NHEAD:
                     head_prep.append(("T", pr))
                     head_prep.append(("C", pr))
                 else:
@@ -180,7 +189,7 @@ def tile_transformerblock_pb_t_kernel(tc, y_act, h, W2, b2, g2, out_0, out_1):
                     plan.setdefault(max(sc, -1), []).append(("C", pr))
             if qs < 0:
                 head_prep.append(("Q", bi))
-            elif bi < 2 or not QG:
+            elif bi < NHEAD or not QG:
                 plan.setdefault(qs, []).append(("Q", bi))
             else:
                 q_at[qs] = bi
@@ -196,7 +205,7 @@ def tile_transformerblock_pb_t_kernel(tc, y_act, h, W2, b2, g2, out_0, out_1):
         w_copy(0)
         w_quant(0)
         w_copy(1)
-        for a in head_prep[:3]:
+        for a in head_prep[:HSPLIT]:
             do_prep(a)
         w_quant(1)
 
@@ -210,7 +219,7 @@ def tile_transformerblock_pb_t_kernel(tc, y_act, h, W2, b2, g2, out_0, out_1):
         nc.scalar.activation(out=b2s[:], in_=b2p[:], func=ACT.Copy, accum_out=sb[:, 0:1])
         nb2h = keep.tile([P, 1], F32, name="nb2h", tag="nb2h")
         nc.scalar.activation(out=nb2h[:, 0:1], in_=sb[:, 0:1], func=ACT.Copy, scale=-1.0 / (2.0 * E))
-        for a in head_prep[3:] + plan.get(-1, []):
+        for a in head_prep[HSPLIT:] + plan.get(-1, []):
             do_prep(a)
 
         r_t = {}
@@ -314,7 +323,6 @@ def tile_transformerblock_pb_t_kernel(tc, y_act, h, W2, b2, g2, out_0, out_1):
         def stage_w(t):
             u_t[t] = u_pool.tile([P, E], F32, name="u_t", tag="u_t")
             nc.gpsimd.tensor_tensor(out=u_t[t][:], in0=r_t[t][:], in1=g2s[:], op=ALU.mult)
-            store_0(t)
 
         def stage_f(t):
             g = t // GROUP
@@ -330,12 +338,12 @@ def tile_transformerblock_pb_t_kernel(tc, y_act, h, W2, b2, g2, out_0, out_1):
                     out=o8[g][:, t % GROUP, :], in_=u_t[t][:], func=ACT.Copy, scale=Y_SCALE, saturate=False
                 )
             casts[g] += 1
-            if g == NG - 1 or casts[g] == GROUP:
+            if g >= TILE_STORES_FROM or casts[g] == GROUP:
                 s1_wait.append(t)
 
         def store_1(t):
             g = t // GROUP
-            if g == NG - 1:
+            if g >= TILE_STORES_FROM:
                 nc.sync.dma_start(out=o1v[g][:, t % GROUP, :], in_=o8[g][:, t % GROUP, :].bitcast(U8))
             else:
                 nc.sync.dma_start(
@@ -393,14 +401,16 @@ def tile_transformerblock_pb_t_kernel(tc, y_act, h, W2, b2, g2, out_0, out_1):
             if is_type(s - LN, "G"):
                 stage_n(s - LN)
                 stage_w(s - LN)
+            if is_type(s - LN - LSG, "G"):
+                store_0(s - LN - LSG)
             for t in s1_wait:
                 store_1(t)
             s1_wait.clear()
             h_upto(min(NT - 1, s + 1 + LEAD))
             for a in plan.get(s, []):
                 do_prep(a)
-            if s < NT and s % GROUP == 1:
-                gl = s // GROUP + PRELOAD
-                if gl < NG:
-                    load_y(gl)
-                    load_h(gl)
+            for kind, g in LATER.get(s, []):
+                if kind == "y":
+                    load_y(g)
+                else:
+                    load_h(g)

@@ -50,6 +50,7 @@ QSTEP = {1: 2, 2: 6, 3: 14, 4: 22}
 TFIRST = {1: 0, 2: 2, 3: 10, 4: 18}
 TPER = {1: 1, 2: 1, 3: 1, 4: 1}
 NHEAD = 1
+TSTEPS = {1: [0, 1], 2: [3, 3, 5, 5], 3: [10, 10, 12, 12], 4: [18, 18, 21, 21]}
 HSPLIT = 5
 LOADS = [("y", 1), ("h", 1), ("y", 2), ("h", 2), ("y", 3), ("h", 3)]
 LATER = {1: [("y", 4), ("h", 4)], 5: [("y", 5), ("h", 5)], 9: [("y", 6), ("h", 6)], 13: [("y", 7), ("h", 7)]}
@@ -180,7 +181,7 @@ def tile_transformerblock_pb_t_kernel(tc, y_act, h, W2, b2, g2, out_0, out_1):
         for bi, b in enumerate(BATCHES):
             qs = QSTEP.get(bi, -1)
             for k, pr in enumerate(b):
-                sc = TFIRST.get(bi, 0) + k // TPER.get(bi, 1)
+                sc = TSTEPS[bi][k] if bi in TSTEPS else 0
                 if bi < NHEAD:
                     head_prep.append(("T", pr))
                     head_prep.append(("C", pr))

from contextlib import ExitStack

import concourse.mybir as mybir
from concourse.masks import make_identity

F32 = mybir.dt.float32
BF16 = mybir.dt.bfloat16
U32 = mybir.dt.uint32
U8 = mybir.dt.uint8
FP8X4 = mybir.dt.float8_e4m3fn_x4
FP8 = mybir.dt.float8_e4m3fn
ALU = mybir.AluOpType
ACT = mybir.ActivationFunctionType

P = 128
K = 512
E = 1024
ROWS = 4096
HALF = 512
NT = ROWS // P
GROUP = 4
NG = NT // GROUP
EPS = 1e-5
Y_SCALE = 220.0
FLOPS = 2 * ROWS * K * E

GMOD = 9
GRES = (2, 4, 6, 8)
GMIN = 2
GMAX = 29
TYPES = ["G" if (t % GMOD in GRES and GMIN <= t <= GMAX) else "V" for t in range(NT)]
LEAD = 3
LFV = 5
LFG = 5
LN = 2
LSG = 0
LO = 4
TILE_STORES_FROM = 7
LS = 1
RB = 10
UB = 9
BATCHES = [[0, 1], [2, 3], [4, 5, 6, 7], [8, 9, 10, 11], [12, 13, 14, 15]]
PRELOAD = 4
QLEAD = 2
QG = False
ML = 1
CL = 1
TLAG = 0
QSTEP = {1: 2, 2: 6, 3: 14, 4: 22}
TFIRST = {1: 0, 2: 2, 3: 10, 4: 18}
TPER = {1: 1, 2: 1, 3: 1, 4: 1}
NHEAD = 1
TSTEPS = {1: [0, 1], 2: [3, 3, 5, 5], 3: [10, 10, 12, 12], 4: [18, 18, 21, 21]}
HSPLIT = 5
LOADS = [("y", 1), ("h", 1), ("y", 2), ("h", 2), ("y", 3), ("h", 3)]
LATER = {1: [("y", 4), ("h", 4)], 5: [("y", 5), ("h", 5)], 9: [("y", 6), ("h", 6)], 13: [("y", 7), ("h", 7)]}
VCAST = (31,)
LVC = 1


def tile_transformerblock_pb_t_kernel(tc, y_act, h, W2, b2, g2, out_0, out_1):
    nc = tc.nc
    yv = y_act.flatten_outer_dims().rearrange("(g p j) k -> g p j k", p=P, j=GROUP)
    hv = h.flatten_outer_dims().rearrange("(g p j) e -> g p j e", p=P, j=GROUP)
    o0v = out_0.flatten_outer_dims().rearrange("(g p j) e -> g p j e", p=P, j=GROUP)
    o1v = out_1.flatten_outer_dims().rearrange("(g p j) e -> g p j e", p=P, j=GROUP)
    wv = W2.rearrange("(p j) e -> p j e", j=4)

    with ExitStack() as ctx:
        keep = ctx.enter_context(tc.tile_pool(name="keep", bufs=1))
        yraw_pool = ctx.enter_context(tc.tile_pool(name="yraw", bufs=8))
        hraw_pool = ctx.enter_context(tc.tile_pool(name="hraw", bufs=5))
        ygrp_pool = ctx.enter_context(tc.tile_pool(name="ygrp", bufs=2))
        ycode_pool = ctx.enter_context(tc.tile_pool(name="ycode", bufs=3))
        r_pool = ctx.enter_context(tc.tile_pool(name="rp", bufs=RB))
        u_pool = ctx.enter_context(tc.tile_pool(name="up", bufs=UB))
        o8_pool = ctx.enter_context(tc.tile_pool(name="o8p", bufs=3))
        sq_pool = ctx.enter_context(tc.tile_pool(name="sqp", bufs=2))
        st_pool = ctx.enter_context(tc.tile_pool(name="stp", bufs=8))
        cst_ps = ctx.enter_context(tc.psum_pool(name="cstps", bufs=1))
        mx_ps = ctx.enter_context(tc.psum_pool(name="mxps", bufs=2))
        tp_ps = ctx.enter_context(tc.psum_pool(name="tpps", bufs=2))
        ctx.enter_context(tc.manual_schedule())

        halves = [slice(0, HALF), slice(HALF, E)]

        bg = keep.tile([P, 2 * E], BF16, name="bg", tag="bg")
        ones = keep.tile([P, P], BF16, name="ones", tag="ones")
        eps_t = keep.tile([P, 1], F32, name="eps_t", tag="eps_t")
        warm = keep.tile([P, 1], F32, name="warm", tag="warm")
        ident = keep.tile([P, P], F32, name="ident", tag="ident")
        nc.vector.memset(bg[:], 0.0)
        nc.vector.memset(ones[:], 1.0)
        nc.vector.memset(eps_t[:], EPS)
        make_identity(nc, ident[:])

        nc.scalar.dma_start(out=bg[0:1, 0:E], in_=b2.rearrange("(o e) -> o e", o=1))
        nc.scalar.dma_start(out=bg[0:1, E : 2 * E], in_=g2.rearrange("(o e) -> o e", o=1))
        nc.scalar.activation(out=warm[:], in_=eps_t[:], func=ACT.Abs_reciprocal_sqrt)

        w_raw = [keep.tile([P, 4, HALF], BF16, name="w_raw%d" % c, tag="w_raw%d" % c) for c in range(2)]
        w_grp = [
            keep.tile([P, HALF, 4], BF16, name="w_grp%d" % c, tag="w_grp%d" % c, align_bytes=64) for c in range(2)
        ]
        w_codes = keep.tile([P, E], U32, name="w_codes", tag="w_codes", align_bytes=64)
        w_scales = keep.tile([P, E], U8, name="w_scales", tag="w_scales", align_bytes=64)

        y_raw = {}
        h_raw = {}

        def load_y(g):
            y_raw[g] = yraw_pool.tile([P, GROUP, K], BF16, name="y_raw", tag="y_raw")
            nc.sync.dma_start(out=y_raw[g][:], in_=yv[g])

        def load_h(g):
            h_raw[g] = hraw_pool.tile([P, GROUP, E], BF16, name="h_raw", tag="h_raw")
            nc.sync.dma_start(out=h_raw[g][:], in_=hv[g])

        y_raw[0] = yraw_pool.tile([P, GROUP, K], BF16, name="y_raw", tag="y_raw")
        h_raw[0] = hraw_pool.tile([P, GROUP, E], BF16, name="h_raw", tag="h_raw")
        nc.sync.dma_start(out=w_raw[0][:], in_=wv[:, :, halves[0]])
        nc.sync.dma_start(out=y_raw[0][:], in_=yv[0])
        nc.sync.dma_start(out=w_raw[1][:], in_=wv[:, :, halves[1]])
        for j in range(GROUP):
            nc.sync.dma_start(out=h_raw[0][:, j, :], in_=hv[0][:, j, :])
        for kind, g in LOADS:
            if kind == "y":
                load_y(g)
            else:
                load_h(g)

        def w_copy(c):
            nc.vector.tensor_copy(out=w_grp[c][:], in_=w_raw[c][:].rearrange("p j w -> p w j"))

        def w_quant(c):
            nc.vector.quantize_mx(
                out=w_codes[:, halves[c]].bitcast(FP8X4),
                scales=w_scales[:, halves[c]],
                in_=w_grp[c][:].rearrange("p w j -> p (w j)"),
            )

        batch_of = {}
        for bi, b in enumerate(BATCHES):
            for k, pr in enumerate(b):
                batch_of[pr] = (bi, k)
        y_grp = {}
        y_codes = {}
        y_scales = {}
        tps = {}

        def prep_pair(pr):
            bi, k = batch_of[pr]
            nb = len(BATCHES[bi])
            if bi not in y_grp:
                y_grp[bi] = ygrp_pool.tile([P, nb * 2 * P * 4], BF16, name="y_grp", tag="y_grp", align_bytes=64)
            tp = tp_ps.tile([P, 2, 2, P], F32, name="tp", tag="tp")
            tps[pr] = tp
            for jj in range(2):
                words = y_raw[pr // 2][:, 2 * (pr % 2) + jj, :].bitcast(F32)
                for u in range(2):
                    nc.tensor.transpose(tp[:, jj, u, :], words[:, u : K // 2 : 2], ident[:])

        def copy_pair(pr):
            bi, k = batch_of[pr]
            tp = tps[pr]
            base = k * 4 * P
            nc.scalar.copy(
                out=y_grp[bi][:].bitcast(F32)[:, base : base + 4 * P].rearrange("p (jj r u) -> p jj r u", jj=2, u=2),
                in_=tp[:].rearrange("p jj u r -> p jj r u"),
            )

        def quantise_batch(bi):
            nb = len(BATCHES[bi])
            y_codes[bi] = ycode_pool.tile([P, nb * 2 * P], U32, name="y_codes", tag="y_codes", align_bytes=64)
            y_scales[bi] = ycode_pool.tile([P, nb * 2 * P], U8, name="y_scales", tag="y_scales", align_bytes=64)
            nc.vector.quantize_mx(out=y_codes[bi][:].bitcast(FP8X4), scales=y_scales[bi][:], in_=y_grp[bi][:])

        plan = {}
        q_at = {}
        head_prep = []
        for bi, b in enumerate(BATCHES):
            qs = QSTEP.get(bi, -1)
            for k, pr in enumerate(b):
                sc = TSTEPS[bi][k] if bi in TSTEPS else 0
                if bi < NHEAD:
                    head_prep.append(("T", pr))
                    head_prep.append(("C", pr))
                else:
                    plan.setdefault(max(sc - TLAG, -1), []).append(("T", pr))
                    plan.setdefault(max(sc, -1), []).append(("C", pr))
            if qs < 0:
                head_prep.append(("Q", bi))
            elif bi < NHEAD or not QG:
                plan.setdefault(qs, []).append(("Q", bi))
            else:
                q_at[qs] = bi

        def do_prep(a):
            if a[0] == "T":
                prep_pair(a[1])
            elif a[0] == "C":
                copy_pair(a[1])
            else:
                quantise_batch(a[1])

        w_copy(0)
        w_quant(0)
        w_copy(1)
        for a in head_prep[:HSPLIT]:
            do_prep(a)
        w_quant(1)

        b2p = cst_ps.tile([P, E], BF16, name="b2p", tag="b2p")
        g2p = cst_ps.tile([P, E], BF16, name="g2p", tag="g2p")
        for c in range(2):
            nc.tensor.matmul(out=b2p[:, halves[c]], lhsT=ones[:], rhs=bg[:, c * HALF : (c + 1) * HALF], start=True, stop=True)

        b2s = keep.tile([P, E], F32, name="b2s", tag="b2s")
        sb = keep.tile([P, 4], F32, name="sb", tag="sb")
        nc.scalar.activation(out=b2s[:], in_=b2p[:], func=ACT.Copy, accum_out=sb[:, 0:1])
        nb2h = keep.tile([P, 1], F32, name="nb2h", tag="nb2h")
        nc.scalar.activation(out=nb2h[:, 0:1], in_=sb[:, 0:1], func=ACT.Copy, scale=-1.0 / (2.0 * E))
        for a in head_prep[HSPLIT:] + plan.get(-1, []):
            do_prep(a)

        r_t = {}
        u_t = {}
        st = {}
        mx = {}
        o8 = {}
        casts = {}
        s1_wait = []
        g2s = keep.tile([P, E], F32, name="g2s", tag="g2s")

        def stage_h(t):
            r_t[t] = r_pool.tile([P, E], F32, name="r_t", tag="r_t")
            nc.gpsimd.tensor_tensor(out=r_t[t][:], in0=h_raw[t // GROUP][:, t % GROUP, :], in1=b2s[:], op=ALU.add)

        def stage_m(t):
            bi, k = batch_of[t // 2]
            cols = slice((2 * k + t % 2) * P, (2 * k + t % 2 + 1) * P)
            mx[t] = []
            for c in range(2):
                acc = mx_ps.tile([P, HALF], F32, name="mx%d" % c, tag="mx%d" % c)
                mx[t].append(acc)
                nc.tensor.matmul_mx(
                    out=acc[:],
                    lhsT=y_codes[bi][:, cols].bitcast(FP8X4),
                    lhsT_scale=y_scales[bi][:, cols],
                    rhs=w_codes[:, halves[c]].bitcast(FP8X4),
                    rhs_scale=w_scales[:, halves[c]],
                    start=True,
                    stop=True,
                )

        def stage_p1(t):
            if TYPES[t] == "V":
                r_t[t] = r_pool.tile([P, E], F32, name="r_t", tag="r_t")
            st[t] = st_pool.tile([P, 8], F32, name="st", tag="st")
            for c in range(2):
                if TYPES[t] == "V":
                    other = h_raw[t // GROUP][:, t % GROUP, halves[c]]
                else:
                    other = r_t[t][:, halves[c]]
                nc.vector.scalar_tensor_tensor(
                    out=r_t[t][:, halves[c]],
                    in0=other,
                    scalar=1.0,
                    in1=mx[t][c][:],
                    op0=ALU.mult,
                    op1=ALU.add,
                    accum_out=st[t][:, c : c + 1],
                )

        def stage_mu(t):
            if TYPES[t] == "V":
                nc.scalar.activation(
                    out=st[t][:, 6:8],
                    in_=st[t][:, 0:2],
                    func=ACT.Identity,
                    scale=-1.0 / E,
                    bias=nb2h[:, 0:1],
                    accum_out=st[t][:, 2:3],
                )
            else:
                nc.scalar.activation(
                    out=st[t][:, 6:8], in_=st[t][:, 0:2], func=ACT.Copy, scale=-1.0 / E, accum_out=st[t][:, 2:3]
                )

        def stage_sq(t):
            junk = sq_pool.tile([P, E], BF16, name="junk", tag="junk")
            if TYPES[t] == "V":
                nc.scalar.activation(out=junk[:], in_=r_t[t][:], func=ACT.Square, accum_out=st[t][:, 3:4])
            else:
                nc.scalar.activation(
                    out=junk[:], in_=r_t[t][:], func=ACT.Square, bias=st[t][:, 2:3], accum_out=st[t][:, 3:4]
                )

        def stage_rs(t):
            nc.scalar.activation(
                out=st[t][:, 5:6], in_=st[t][:, 3:4], func=ACT.Abs_reciprocal_sqrt, scale=1.0 / E, bias=eps_t[:, 0:1]
            )

        def stage_s2(t):
            nc.vector.scalar_tensor_tensor(
                out=r_t[t][:], in0=r_t[t][:], scalar=st[t][:, 2:3], in1=b2p[:], op0=ALU.add, op1=ALU.add
            )

        def store_0(t):
            nc.sync.dma_start(out=o0v[t // GROUP][:, t % GROUP, :], in_=u_t[t][:])

        def stage_o(t):
            u_t[t] = u_pool.tile([P, E], F32, name="u_t", tag="u_t")
            nc.vector.scalar_tensor_tensor(
                out=u_t[t][:], in0=r_t[t][:], scalar=st[t][:, 5:6], in1=g2p[:], op0=ALU.mult, op1=ALU.mult
            )
            store_0(t)

        def stage_n(t):
            nc.gpsimd.tensor_scalar(
                out=r_t[t][:], in0=r_t[t][:], scalar1=st[t][:, 2:3], scalar2=st[t][:, 5:6], op0=ALU.add, op1=ALU.mult
            )

        def stage_w(t):
            u_t[t] = u_pool.tile([P, E], F32, name="u_t", tag="u_t")
            nc.gpsimd.tensor_tensor(out=u_t[t][:], in0=r_t[t][:], in1=g2s[:], op=ALU.mult)

        def stage_f(t):
            g = t // GROUP
            if g not in o8:
                o8[g] = o8_pool.tile([P, GROUP, E], FP8, name="o8", tag="o8")
                casts[g] = 0
            if t in VCAST:
                nc.vector.tensor_scalar(
                    out=o8[g][:, t % GROUP, :], in0=u_t[t][:], scalar1=Y_SCALE, scalar2=None, op0=ALU.mult, saturate=False
                )
            else:
                nc.scalar.activation(
                    out=o8[g][:, t % GROUP, :], in_=u_t[t][:], func=ACT.Copy, scale=Y_SCALE, saturate=False
                )
            casts[g] += 1
            if g >= TILE_STORES_FROM or casts[g] == GROUP:
                s1_wait.append(t)

        def store_1(t):
            g = t // GROUP
            if g >= TILE_STORES_FROM:
                nc.sync.dma_start(out=o1v[g][:, t % GROUP, :], in_=o8[g][:, t % GROUP, :].bitcast(U8))
            else:
                nc.sync.dma_start(
                    out=o1v[g].rearrange("p j e -> p (j e)"), in_=o8[g][:].rearrange("p j e -> p (j e)").bitcast(U8)
                )

        g_tiles = [t for t in range(NT) if TYPES[t] == "G"]
        h_done = [0]

        def h_upto(t):
            while h_done[0] < len(g_tiles) and g_tiles[h_done[0]] <= t:
                stage_h(g_tiles[h_done[0]])
                h_done[0] += 1

        def is_type(t, kind):
            return 0 <= t < NT and TYPES[t] == kind

        stage_m(0)
        for c in range(2):
            nc.tensor.matmul(
                out=g2p[:, halves[c]], lhsT=ones[:], rhs=bg[:, E + c * HALF : E + (c + 1) * HALF], start=True, stop=True
            )
        nc.scalar.copy(out=g2s[:], in_=g2p[:])
        for t in range(1, ML):
            stage_m(t)
        pend = []
        for s in range(NT + max(LFG, LFV) + 1):
            if s == 0:
                h_upto(LEAD)
            if s < NT:
                stage_p1(s)
                if s in q_at:
                    quantise_batch(q_at[s])
                if s + ML < NT:
                    stage_m(s + ML)
                stage_mu(s)
            for t in pend:
                stage_rs(t)
            pend.clear()
            if is_type(s - LFV, "V") and s - LFV not in VCAST:
                stage_f(s - LFV)
            if is_type(s - LFG, "G"):
                stage_f(s - LFG)
            if is_type(s - LS, "V"):
                stage_s2(s - LS)
                stage_sq(s - LS)
                pend.append(s - LS)
            if is_type(s, "G"):
                stage_sq(s)
                pend.append(s)
            if is_type(s - LO, "V"):
                stage_o(s - LO)
            if s - LO - LVC in VCAST:
                stage_f(s - LO - LVC)
            if is_type(s - LN, "G"):
                stage_n(s - LN)
                stage_w(s - LN)
            if is_type(s - LN - LSG, "G"):
                store_0(s - LN - LSG)
            for t in s1_wait:
                store_1(t)
            s1_wait.clear()
            h_upto(min(NT - 1, s + 1 + LEAD))
            for a in plan.get(s, []):
                do_prep(a)
            for kind, g in LATER.get(s, []):
                if kind == "y":
                    load_y(g)
                else:
                    load_h(g)
